import numpy as np
import ml_dtypes


def mxq(x, axis, fmt="e4m3"):
    dtype, down = {"e4m3": (ml_dtypes.float8_e4m3fn, 7), "e5m2": (ml_dtypes.float8_e5m2, 14)}[fmt]
    v = np.moveaxis(np.asarray(x, np.float32).astype(ml_dtypes.bfloat16).astype(np.float64), axis, -1)
    blocks = v.reshape(v.shape[:-1] + (-1, 32))
    amax = np.abs(blocks).max(-1, keepdims=True)
    byte = np.maximum(np.where(amax > 0, np.frexp(amax)[1] - 1 + 127, 0) - down, 1)
    scale = np.exp2(byte - 127.0)
    codes = (blocks / scale).astype(np.float32).astype(dtype).astype(np.float64)
    return np.moveaxis((codes * scale).reshape(v.shape), -1, axis)


WIDE = False


def mx_kscale(k):
    if not WIDE:
        return np.ones(k)
    levels = np.array([10, -10, 5, -5, 0])
    a = np.random.permutation(np.resize(levels, k // 512 * 4)).reshape(k // 512, 4)
    idx = np.arange(k)
    return np.exp2(a[idx // 512, idx % 128 // 32])


BF16 = ml_dtypes.bfloat16


def bf(x):
    return np.asarray(x, np.float32).astype(BF16)


def f64(x):
    return np.asarray(x).astype(np.float64)


E2M1 = np.array([0.0, 0.5, 1.0, 1.5, 2.0, 3.0, 4.0, 6.0, -0.0, -0.5, -1.0, -1.5, -2.0, -3.0, -4.0, -6.0])


def pack_weight(w, fmt):
    k, n = w.shape
    w = f64(bf(w)).reshape(k // 32, 32, n)
    amax = np.abs(w).max(1)
    if fmt == "e4m3":
        byte = np.frexp(amax)[1] - 1 + 127 - 7
    else:
        mant, ex = np.frexp(amax / 6.0)
        byte = np.where(mant > 0.5, ex, ex - 1) + 127
    byte = np.clip(np.where(amax > 0, byte, 1), 1, 254)
    scaled = (w * np.exp2(127.0 - byte)[:, None, :]).reshape(k, n).astype(np.float32)
    by_word = np.ascontiguousarray(scaled.reshape(k // 512, 128, 4, n).transpose(0, 1, 3, 2))
    if fmt == "e4m3":
        words = by_word.astype(ml_dtypes.float8_e4m3fn).view(np.uint8)
    else:
        c = by_word.astype(ml_dtypes.float4_e2m1fn).view(np.uint8) & 0xF
        words = c[..., 0::2] | (c[..., 1::2] << 4)
    return np.ascontiguousarray(words), np.ascontiguousarray(byte.astype(np.uint8).reshape(k // 512, 16, n))


def unpack_weight(words, scales, fmt):
    g, p, n, _ = words.shape
    if fmt == "e4m3":
        vals = np.ascontiguousarray(words).view(ml_dtypes.float8_e4m3fn).astype(np.float64)
    else:
        nib = np.empty((g, p, n, 4), np.uint8)
        nib[..., 0::2] = words & 0xF
        nib[..., 1::2] = words >> 4
        vals = E2M1[nib]
    vals = vals * np.repeat(np.exp2(scales.astype(np.float64) - 127.0), 8, axis=1)[..., None]
    return vals.transpose(0, 1, 3, 2).reshape(g * 512, n)


B, F, C, H = 2, 1024, 512, 512
K = C + H
FMT = "e4m3"


def sigmoid(v):
    return 1.0 / (1.0 + np.exp(-v))


def setup_inputs():
    s = mx_kscale(K)

    def w():
        return pack_weight(np.ascontiguousarray((np.random.standard_normal((H, K)) / np.sqrt(K) / s[None, :]).T), FMT)

    def b():
        return bf(np.random.standard_normal(H) * 0.3)

    x = bf(np.random.standard_normal((B, F, C)) * s[None, None, :C])
    hidden_state = bf(np.random.standard_normal((B, H, F)) * s[None, C:, None])
    cell_state = bf(np.random.standard_normal((B, H, F)))
    W_f_words, W_f_scales = w()
    b_f = b()
    W_i_words, W_i_scales = w()
    b_i = b()
    W_o_words, W_o_scales = w()
    b_o = b()
    W_g_words, W_g_scales = w()
    b_g = b()
    return {"x": x,
            "hidden_state": hidden_state,
            "cell_state": cell_state,
            "W_f_words": W_f_words, "W_f_scales": W_f_scales, "b_f": b_f,
            "W_i_words": W_i_words, "W_i_scales": W_i_scales, "b_i": b_i,
            "W_o_words": W_o_words, "W_o_scales": W_o_scales, "b_o": b_o,
            "W_g_words": W_g_words, "W_g_scales": W_g_scales, "b_g": b_g}


def reference(x, hidden_state, cell_state, W_f_words, W_f_scales, b_f, W_i_words, W_i_scales, b_i, W_o_words, W_o_scales, b_o, W_g_words, W_g_scales, b_g):
    xh = np.concatenate([np.swapaxes(f64(x), 1, 2), f64(hidden_state)], axis=1)
    W = np.concatenate([unpack_weight(W_f_words, W_f_scales, FMT).T,
                        unpack_weight(W_i_words, W_i_scales, FMT).T,
                        unpack_weight(W_g_words, W_g_scales, FMT).T,
                        unpack_weight(W_o_words, W_o_scales, FMT).T], axis=0)
    b = np.concatenate([f64(b_f), f64(b_i), f64(b_g), f64(b_o)], axis=0)
    gates = (W @ mxq(xh, 1, "e4m3")) + b[None, :, None]
    f_t = sigmoid(gates[:, 0 * H:1 * H])
    i_t = sigmoid(gates[:, 1 * H:2 * H])
    g_t = np.tanh(gates[:, 2 * H:3 * H])
    o_t = sigmoid(gates[:, 3 * H:4 * H])
    new_cell = f64(cell_state) * f_t + i_t * g_t
    new_hidden = np.tanh(new_cell) * o_t
    return (np.swapaxes(new_hidden, 1, 2), new_hidden, new_cell)

@@ -1,0 +1,331 @@
+from contextlib import ExitStack
+
+import concourse.mybir as mybir
+from concourse.masks import make_identity
+
+F32 = mybir.dt.float32
+BF16 = mybir.dt.bfloat16
+I32 = mybir.dt.int32
+U32 = mybir.dt.uint32
+U8 = mybir.dt.uint8
+FP8X4 = mybir.dt.float8_e4m3fn_x4
+ACT = mybir.ActivationFunctionType
+ALU = mybir.AluOpType
+
+P = 128
+PACK = 4
+BATCH, POSITIONS, CHANNELS, HIDDEN = 2, 1024, 512, 512
+PASSES = 2
+PASS_ORDER = (1, 0)
+TILE = 512
+TILES_PER_BATCH = POSITIONS // TILE
+TILES = BATCH * TILES_PER_BATCH
+H_BLOCKS = HIDDEN // P
+UNITS = TILES * H_BLOCKS
+ROW_BLOCKS = TILE // P
+HALF = TILE // 2
+GATES = ("f", "i", "g", "o")
+GATE_FUNC = {"f": ACT.Sigmoid, "i": ACT.Sigmoid, "g": ACT.Tanh, "o": ACT.Sigmoid}
+QUADRANTS = 4
+PREPARE_AHEAD = 4
+LOAD_AHEAD = 3
+W_PART = 256
+
+FLOPS = 2 * len(GATES) * HIDDEN * (CHANNELS + HIDDEN) * BATCH * POSITIONS
+
+
+def tile_batchedlstm_kernel(
+    tc,
+    x,
+    hidden_state,
+    cell_state,
+    W_f_words,
+    W_f_scales,
+    b_f,
+    W_i_words,
+    W_i_scales,
+    b_i,
+    W_o_words,
+    W_o_scales,
+    b_o,
+    W_g_words,
+    W_g_scales,
+    b_g,
+    out_0,
+    out_1,
+    out_2,
+):
+    nc = tc.nc
+    words_in = {"f": W_f_words, "i": W_i_words, "g": W_g_words, "o": W_o_words}
+    scales_in = {"f": W_f_scales, "i": W_i_scales, "g": W_g_scales, "o": W_o_scales}
+    bias_in = {"f": b_f, "i": b_i, "g": b_g, "o": b_o}
+
+    with ExitStack() as ctx:
+        keep = ctx.enter_context(tc.tile_pool(name="keep", bufs=1))
+        work = ctx.enter_context(tc.tile_pool(name="work", bufs=2))
+        gate_psum = ctx.enter_context(tc.psum_pool(name="gate_psum", bufs=5))
+        turn_psum = ctx.enter_context(tc.psum_pool(name="turn_psum", bufs=3))
+        ctx.enter_context(tc.manual_schedule())
+
+        def where(tile_index):
+            return tile_index // TILES_PER_BATCH, (tile_index % TILES_PER_BATCH) * TILE
+
+        x_rows = {
+            (n, half): keep.tile([P, HALF // P, CHANNELS], BF16, name="x_rows%d%d" % (n, half))
+            for n in range(TILES)
+            for half in range(2)
+        }
+        hidden_rows = [keep.tile([P, PACK, TILE], BF16, name="hidden_rows%d" % n) for n in range(TILES)]
+        xh_codes = [keep.tile([P, PASSES, TILE], U32, name="xh_codes%d" % n, align_bytes=64) for n in range(TILES)]
+        xh_scales = [keep.tile([P, PASSES, TILE], U8, name="xh_scales%d" % n, align_bytes=64) for n in range(TILES)]
+        cell_rows = {
+            (b, hb): keep.tile([P, POSITIONS], BF16, name="cell_rows%d%d" % (b, hb))
+            for b in range(BATCH)
+            for hb in range(H_BLOCKS)
+        }
+        w_codes = {
+            (gate, part): keep.tile([P, PASSES, W_PART], U32, name="w_codes_%s%d" % (gate, part), align_bytes=64)
+            for gate in GATES
+            for part in range(HIDDEN // W_PART)
+        }
+        w_scales = {gate: keep.tile([P, HIDDEN], U8, name="w_scales_%s" % gate, align_bytes=64) for gate in GATES}
+
+        def load_x(n, half):
+            b, f0 = where(n)
+            first = f0 + half * HALF
+            nc.sync.dma_start(out=x_rows[n, half][:], in_=x[b, first : first + HALF, :].rearrange("(j p) c -> p j c", p=P))
+
+        def load_hidden(n):
+            b, f0 = where(n)
+            nc.sync.dma_start(
+                out=hidden_rows[n][:],
+                in_=hidden_state[b, :, f0 : f0 + TILE].rearrange("(p t) f -> p t f", t=PACK),
+            )
+
+        def load_weight_scales(gate):
+            for quadrant in range(QUADRANTS):
+                nc.sync.dma_start(
+                    out=w_scales[gate][32 * quadrant : 32 * quadrant + PASSES * 4, :].bitcast(I32),
+                    in_=scales_in[gate][:, 4 * quadrant : 4 * quadrant + 4, :].bitcast(I32),
+                )
+
+        def load_weight_codes(gate, part):
+            all_bytes = words_in[gate].rearrange("c p n t -> p c (n t)")
+            nc.sync.dma_start(
+                out=w_codes[gate, part][:].bitcast(I32),
+                in_=all_bytes[:, :, part * W_PART * PACK : (part + 1) * W_PART * PACK].bitcast(I32),
+            )
+
+        def load_cell(b, hb):
+            nc.sync.dma_start(out=cell_rows[b, hb][:], in_=cell_state[b, hb * P : (hb + 1) * P, :])
+
+        grouped_x = {}
+        grouped_hidden = {}
+        turned_x = {}
+
+        def turn_x(n, half):
+            bank = turn_psum.tile([P, 2, 2, P], F32, tag="turn", name="turned_x")
+            for j in range(2):
+                words = x_rows[n, half][:, j, :].bitcast(F32)
+                for u in range(2):
+                    nc.tensor.transpose(bank[:, j, u, :], words[:, u : CHANNELS // 2 : 2], identity[:])
+            turned_x[n, half] = bank
+
+        def copy_x(n, half):
+            if half == 0:
+                grouped_x[n] = work.tile([P, TILE, PACK], BF16, name="grouped_x", align_bytes=64)
+            as_words = grouped_x[n][:].bitcast(F32).rearrange("p (j f) u -> p j f u", f=P)
+            nc.scalar.copy(
+                out=as_words[:, 2 * half : 2 * half + 2, :, :],
+                in_=turned_x[n, half][:].rearrange("p j u f -> p j f u"),
+            )
+
+        def regroup_hidden(n, half):
+            if half == 0:
+                grouped_hidden[n] = work.tile([P, TILE, PACK], BF16, name="grouped_hidden", align_bytes=64)
+            columns = slice(half * HALF, (half + 1) * HALF)
+            nc.vector.tensor_copy(
+                out=grouped_hidden[n][:, columns, :].rearrange("p (c i) t -> p c t i", i=4),
+                in_=hidden_rows[n][:, :, columns].rearrange("p t (c i) -> p c t i", i=4),
+            )
+
+        def quantise(n, c, grouped):
+            nc.vector.quantize_mx(
+                out=xh_codes[n][:, c, :].bitcast(FP8X4),
+                scales=xh_scales[n][:, c, :],
+                in_=grouped[:].rearrange("p f t -> p (f t)"),
+            )
+
+        pre = {}
+        gate_out = {}
+        kept = {}
+        fresh = {}
+        tanh_cell = {}
+        new_cell = {}
+        new_hidden = {}
+        turned_hidden = {}
+
+        def multiply(u):
+            n, hb = divmod(u, H_BLOCKS)
+            part, first = divmod(hb * P, W_PART)
+            for gate in GATES:
+                pre[u, gate] = gate_psum.tile([P, TILE], F32, tag="pre", name="pre_" + gate)
+                for c in PASS_ORDER:
+                    nc.tensor.matmul_mx(
+                        out=pre[u, gate][:],
+                        lhsT=w_codes[gate, part][:, c, first : first + P].bitcast(FP8X4),
+                        lhsT_scale=w_scales[gate][4 * c : P, hb * P : (hb + 1) * P],
+                        rhs=xh_codes[n][:, c, :].bitcast(FP8X4),
+                        rhs_scale=xh_scales[n][:, c, :],
+                        start=(c == PASS_ORDER[0]),
+                        stop=(c == PASS_ORDER[-1]),
+                    )
+
+        def activate(u, gate):
+            hb = u % H_BLOCKS
+            column = GATES.index(gate) * H_BLOCKS + hb
+            gate_out[u, gate] = work.tile([P, TILE], F32, name="gate_" + gate, bufs=3)
+            nc.scalar.activation(
+                out=gate_out[u, gate][:],
+                in_=pre[u, gate][:],
+                func=GATE_FUNC[gate],
+                bias=bias_columns[:, column : column + 1],
+                scale=1.0,
+            )
+
+        def keep_old_cell(u):
+            n, hb = divmod(u, H_BLOCKS)
+            b, f0 = where(n)
+            kept[u] = work.tile([P, TILE], F32, name="kept")
+            nc.vector.tensor_tensor(
+                out=kept[u][:], in0=gate_out[u, "f"][:], in1=cell_rows[b, hb][:, f0 : f0 + TILE], op=ALU.mult
+            )
+
+        def make_fresh(u):
+            fresh[u] = work.tile([P, TILE], F32, name="fresh")
+            nc.vector.tensor_tensor(out=fresh[u][:], in0=gate_out[u, "i"][:], in1=gate_out[u, "g"][:], op=ALU.mult)
+
+        def finish_cell(u):
+            n, hb = divmod(u, H_BLOCKS)
+            b, f0 = where(n)
+            new_cell[u] = work.tile([P, TILE], F32, name="new_cell", bufs=3)
+            nc.vector.tensor_tensor(out=new_cell[u][:], in0=kept[u][:], in1=fresh[u][:], op=ALU.add)
+            nc.sync.dma_start(out=out_2[b, hb * P : (hb + 1) * P, f0 : f0 + TILE], in_=new_cell[u][:])
+
+        def squash_cell(u):
+            tanh_cell[u] = work.tile([P, TILE], F32, name="tanh_cell")
+            nc.scalar.activation(out=tanh_cell[u][:], in_=new_cell[u][:], func=ACT.Tanh)
+
+        def finish_hidden(u):
+            n, hb = divmod(u, H_BLOCKS)
+            b, f0 = where(n)
+            new_hidden[u] = work.tile([P, TILE], F32, name="new_hidden", bufs=3)
+            nc.vector.tensor_tensor(out=new_hidden[u][:], in0=gate_out[u, "o"][:], in1=tanh_cell[u][:], op=ALU.mult)
+            nc.sync.dma_start(out=out_1[b, hb * P : (hb + 1) * P, f0 : f0 + TILE], in_=new_hidden[u][:])
+
+        def turn_hidden(u):
+            turned_hidden[u] = turn_psum.tile([P, ROW_BLOCKS, P], F32, tag="turn", name="turned_hidden")
+            for j in range(ROW_BLOCKS):
+                nc.tensor.transpose(turned_hidden[u][:, j, :], new_hidden[u][:, j * P : (j + 1) * P], identity[:])
+
+        def copy_turned_hidden(u):
+            n, hb = divmod(u, H_BLOCKS)
+            b, f0 = where(n)
+            by_position = work.tile([P, ROW_BLOCKS, P], F32, name="by_position", bufs=3)
+            nc.vector.tensor_copy(out=by_position[:], in_=turned_hidden[u][:])
+            nc.sync.dma_start(
+                out=out_0[b, f0 : f0 + TILE, hb * P : (hb + 1) * P].rearrange("(j p) h -> p j h", p=P), in_=by_position[:]
+            )
+
+        bias_rows = keep.tile([P, P], BF16, name="bias_rows")
+        nc.vector.memset(bias_rows[:], 0.0)
+        for gate in GATES:
+            nc.vector.memset(w_scales[gate][:].bitcast(I32), 0)
+        identity = keep.tile([P, P], F32, name="identity")
+        make_identity(nc, identity[:])
+        identity_bf16 = keep.tile([P, P], BF16, name="identity_bf16")
+
+        for row, gate in enumerate(GATES):
+            nc.gpsimd.dma_start(
+                out=bias_rows[row * H_BLOCKS : (row + 1) * H_BLOCKS, :], in_=bias_in[gate].rearrange("(hb h) -> hb h", h=P)
+            )
+        make_identity(nc, identity_bf16[:])
+        warm = keep.tile([P, 1], F32, name="warm")
+        nc.vector.memset(warm[:], 0.0)
+        nc.scalar.activation(out=warm[:], in_=warm[:], func=ACT.Sigmoid)
+
+        load_x(0, 0)
+        load_x(0, 1)
+        load_hidden(0)
+        for gate in GATES:
+            load_weight_scales(gate)
+            load_weight_codes(gate, 0)
+        load_cell(0, 0)
+        load_hidden(1)
+        load_x(1, 0)
+        load_x(1, 1)
+        load_cell(0, 1)
+        for gate in GATES:
+            load_weight_codes(gate, 1)
+        load_cell(0, 2)
+        load_cell(0, 3)
+
+        turn_x(0, 0)
+        copy_x(0, 0)
+        turn_x(0, 1)
+        copy_x(0, 1)
+        regroup_hidden(0, 0)
+        regroup_hidden(0, 1)
+
+        turned_bias = turn_psum.tile([P, P], BF16, tag="turn", name="turned_bias")
+        nc.tensor.transpose(turned_bias[:], bias_rows[:], identity_bf16[:])
+
+        quantise(0, 1, grouped_hidden[0])
+        quantise(0, 0, grouped_x[0])
+        bias_columns = keep.tile([P, len(GATES) * H_BLOCKS], F32, name="bias_columns")
+        nc.vector.tensor_copy(out=bias_columns[:], in_=turned_bias[:, 0 : len(GATES) * H_BLOCKS])
+
+        for u in range(-1, UNITS + 3):
+            next_tile, quarter = divmod(u + PREPARE_AHEAD, H_BLOCKS)
+            preparing = 1 <= next_tile < TILES
+            tile_to_load, load_quarter = divmod(u + PREPARE_AHEAD + LOAD_AHEAD, H_BLOCKS)
+            unit_to_load = u + LOAD_AHEAD
+
+            if load_quarter == 0 and 2 <= tile_to_load < TILES:
+                load_hidden(tile_to_load)
+                load_x(tile_to_load, 0)
+                load_x(tile_to_load, 1)
+            if UNITS // BATCH <= unit_to_load < UNITS // BATCH + H_BLOCKS:
+                load_cell(1, unit_to_load % H_BLOCKS)
+
+            if 0 <= u - 1 < UNITS:
+                finish_cell(u - 1)
+            if 0 <= u < UNITS:
+                activate(u, "f")
+            if 0 <= u - 2 < UNITS:
+                finish_hidden(u - 2)
+            if 0 <= u < UNITS:
+                activate(u, "i")
+                keep_old_cell(u)
+                activate(u, "g")
+            if preparing and quarter in (1, 2):
+                copy_x(next_tile, quarter - 1)
+            if preparing and quarter in (0, 1):
+                regroup_hidden(next_tile, quarter)
+            if preparing and quarter == 2:
+                quantise(next_tile, 1, grouped_hidden[next_tile])
+            if preparing and quarter == 3:
+                quantise(next_tile, 0, grouped_x[next_tile])
+            if u + 1 < UNITS:
+                multiply(u + 1)
+            if 0 <= u - 2 < UNITS:
+                turn_hidden(u - 2)
+            if preparing and quarter in (0, 1):
+                turn_x(next_tile, quarter)
+            if 0 <= u < UNITS:
+                activate(u, "o")
+                make_fresh(u)
+            if 0 <= u - 1 < UNITS:
+                squash_cell(u - 1)
+            if 0 <= u - 3 < UNITS:
+                copy_turned_hidden(u - 3)

@@ -256,8 +256,10 @@ def tile_batchedlstm_kernel(
 
         load_x(0, 0)
         load_x(0, 1)
+        load_weight_scales("f")
+        load_weight_codes("f", 0)
         load_hidden(0)
-        for gate in GATES:
+        for gate in ("i", "g", "o"):
             load_weight_scales(gate)
             load_weight_codes(gate, 0)
         load_cell(0, 0)
@@ -298,6 +300,12 @@ def tile_batchedlstm_kernel(
             if UNITS // BATCH <= unit_to_load < UNITS // BATCH + H_BLOCKS:
                 load_cell(1, unit_to_load % H_BLOCKS)
 
+            if preparing and quarter in (0, 1):
+                regroup_hidden(next_tile, quarter)
+            if preparing and quarter == 2:
+                quantise(next_tile, 1, grouped_hidden[next_tile])
+            if preparing and quarter == 3:
+                quantise(next_tile, 0, grouped_x[next_tile])
             if 0 <= u - 1 < UNITS:
                 finish_cell(u - 1)
             if 0 <= u < UNITS:
@@ -310,12 +318,6 @@ def tile_batchedlstm_kernel(
                 activate(u, "g")
             if preparing and quarter in (1, 2):
                 copy_x(next_tile, quarter - 1)
-            if preparing and quarter in (0, 1):
-                regroup_hidden(next_tile, quarter)
-            if preparing and quarter == 2:
-                quantise(next_tile, 1, grouped_hidden[next_tile])
-            if preparing and quarter == 3:
-                quantise(next_tile, 0, grouped_x[next_tile])
             if u + 1 < UNITS:
                 multiply(u + 1)
             if 0 <= u - 2 < UNITS:

@@ -29,6 +29,7 @@ GATE_FUNC = {"f": ACT.Sigmoid, "i": ACT.Sigmoid, "g": ACT.Tanh, "o": ACT.Sigmoid
 QUADRANTS = 4
 PREPARE_AHEAD = 4
 LOAD_AHEAD = 3
+WARM_AT_START = 4
 W_PART = 256
 
 FLOPS = 2 * len(GATES) * HIDDEN * (CHANNELS + HIDDEN) * BATCH * POSITIONS
@@ -237,6 +238,15 @@ def tile_batchedlstm_kernel(
                 out=out_0[b, f0 : f0 + TILE, hb * P : (hb + 1) * P].rearrange("(j p) h -> p j h", p=P), in_=by_position[:]
             )
 
+        zeros = keep.tile([P, TILE], BF16, name="zeros")
+        nc.vector.memset(zeros[:], 0.0)
+        idle_bank = gate_psum.tile([P, TILE], F32, tag="pre", name="idle_bank")
+
+        def keep_warm(moving, count):
+            for k in range(count):
+                nc.tensor.matmul(out=idle_bank[:], lhsT=zeros[:, 0:P], rhs=moving, start=True, stop=True)
+
+        keep_warm(zeros[:], WARM_AT_START)
         bias_rows = keep.tile([P, P], BF16, name="bias_rows")
         nc.vector.memset(bias_rows[:], 0.0)
         for gate in GATES:
@@ -272,12 +282,19 @@ def tile_batchedlstm_kernel(
         load_cell(0, 2)
         load_cell(0, 3)
 
+        def quarter_of(grouped, half):
+            return grouped[:, half * HALF : half * HALF + TILE // PACK, :].rearrange("p f t -> p (f t)")
+
         turn_x(0, 0)
         copy_x(0, 0)
         turn_x(0, 1)
         copy_x(0, 1)
+        keep_warm(quarter_of(grouped_x[0], 0), 2)
+        keep_warm(quarter_of(grouped_x[0], 1), 2)
         regroup_hidden(0, 0)
         regroup_hidden(0, 1)
+        keep_warm(quarter_of(grouped_hidden[0], 0), 2)
+        keep_warm(quarter_of(grouped_hidden[0], 1), 2)
 
         turned_bias = turn_psum.tile([P, P], BF16, tag="turn", name="turned_bias")
         nc.tensor.transpose(turned_bias[:], bias_rows[:], identity_bf16[:])

@@ -28,8 +28,9 @@ GATES = ("f", "i", "g", "o")
 GATE_FUNC = {"f": ACT.Sigmoid, "i": ACT.Sigmoid, "g": ACT.Tanh, "o": ACT.Sigmoid}
 QUADRANTS = 4
 PREPARE_AHEAD = 4
-LOAD_AHEAD = 3
+LOAD_AHEAD = 5
 WARM_AT_START = 4
+SPLIT_COPIES = (0, 2, 4, 6, 8)
 W_PART = 256
 
 FLOPS = 2 * len(GATES) * HIDDEN * (CHANNELS + HIDDEN) * BATCH * POSITIONS
@@ -124,13 +125,17 @@ def tile_batchedlstm_kernel(
         grouped_hidden = {}
         turned_x = {}
 
+        def turn_x_block(n, block):
+            half, j = divmod(block, 2)
+            if j == 0:
+                turned_x[n, half] = turn_psum.tile([P, 2, 2, P], F32, tag="turn", name="turned_x")
+            words = x_rows[n, half][:, j, :].bitcast(F32)
+            for u in range(2):
+                nc.tensor.transpose(turned_x[n, half][:, j, u, :], words[:, u : CHANNELS // 2 : 2], identity[:])
+
         def turn_x(n, half):
-            bank = turn_psum.tile([P, 2, 2, P], F32, tag="turn", name="turned_x")
-            for j in range(2):
-                words = x_rows[n, half][:, j, :].bitcast(F32)
-                for u in range(2):
-                    nc.tensor.transpose(bank[:, j, u, :], words[:, u : CHANNELS // 2 : 2], identity[:])
-            turned_x[n, half] = bank
+            turn_x_block(n, 2 * half)
+            turn_x_block(n, 2 * half + 1)
 
         def copy_x(n, half):
             if half == 0:
@@ -233,7 +238,11 @@ def tile_batchedlstm_kernel(
             n, hb = divmod(u, H_BLOCKS)
             b, f0 = where(n)
             by_position = work.tile([P, ROW_BLOCKS, P], F32, name="by_position", bufs=3)
-            nc.vector.tensor_copy(out=by_position[:], in_=turned_hidden[u][:])
+            if u in SPLIT_COPIES:
+                nc.scalar.copy(out=by_position[:, 0:2, :], in_=turned_hidden[u][:, 0:2, :])
+                nc.vector.tensor_copy(out=by_position[:, 2:4, :], in_=turned_hidden[u][:, 2:4, :])
+            else:
+                nc.vector.tensor_copy(out=by_position[:], in_=turned_hidden[u][:])
             nc.sync.dma_start(
                 out=out_0[b, f0 : f0 + TILE, hb * P : (hb + 1) * P].rearrange("(j p) h -> p j h", p=P), in_=by_position[:]
             )
@@ -333,14 +342,19 @@ def tile_batchedlstm_kernel(
                 activate(u, "i")
                 keep_old_cell(u)
                 activate(u, "g")
-            if preparing and quarter in (1, 2):
-                copy_x(next_tile, quarter - 1)
+            if next_tile == 1 and quarter in (1, 2):
+                copy_x(1, quarter - 1)
+            if 2 <= next_tile < TILES and quarter in (0, 2):
+                copy_x(next_tile, quarter // 2)
             if u + 1 < UNITS:
                 multiply(u + 1)
             if 0 <= u - 2 < UNITS:
                 turn_hidden(u - 2)
-            if preparing and quarter in (0, 1):
-                turn_x(next_tile, quarter)
+            if next_tile == 1 and quarter in (0, 1):
+                turn_x(1, quarter)
+            tile_to_turn, block = divmod(u + PREPARE_AHEAD + 2, H_BLOCKS)
+            if 2 <= tile_to_turn < TILES:
+                turn_x_block(tile_to_turn, block)
             if 0 <= u < UNITS:
                 activate(u, "o")
                 make_fresh(u)

@@ -190,7 +190,7 @@ def tile_batchedlstm_kernel(
         def activate(u, gate):
             hb = u % H_BLOCKS
             column = GATES.index(gate) * H_BLOCKS + hb
-            gate_out[u, gate] = work.tile([P, TILE], F32, name="gate_" + gate, bufs=3)
+            gate_out[u, gate] = work.tile([P, TILE], F32, name="gate_" + gate, bufs=4)
             nc.scalar.activation(
                 out=gate_out[u, gate][:],
                 in_=pre[u, gate][:],
@@ -202,34 +202,45 @@ def tile_batchedlstm_kernel(
         def keep_old_cell(u):
             n, hb = divmod(u, H_BLOCKS)
             b, f0 = where(n)
-            kept[u] = work.tile([P, TILE], F32, name="kept")
+            kept[u] = work.tile([P, TILE], F32, name="kept", bufs=4)
             nc.vector.tensor_tensor(
                 out=kept[u][:], in0=gate_out[u, "f"][:], in1=cell_rows[b, hb][:, f0 : f0 + TILE], op=ALU.mult
             )
 
         def make_fresh(u):
-            fresh[u] = work.tile([P, TILE], F32, name="fresh")
+            fresh[u] = work.tile([P, TILE], F32, name="fresh", bufs=4)
             nc.vector.tensor_tensor(out=fresh[u][:], in0=gate_out[u, "i"][:], in1=gate_out[u, "g"][:], op=ALU.mult)
 
         def finish_cell(u):
             n, hb = divmod(u, H_BLOCKS)
             b, f0 = where(n)
-            new_cell[u] = work.tile([P, TILE], F32, name="new_cell", bufs=3)
+            new_cell[u] = work.tile([P, TILE], F32, name="new_cell", bufs=5)
             nc.vector.tensor_tensor(out=new_cell[u][:], in0=kept[u][:], in1=fresh[u][:], op=ALU.add)
             nc.sync.dma_start(out=out_2[b, hb * P : (hb + 1) * P, f0 : f0 + TILE], in_=new_cell[u][:])
 
         def squash_cell(u):
-            tanh_cell[u] = work.tile([P, TILE], F32, name="tanh_cell")
+            tanh_cell[u] = work.tile([P, TILE], F32, name="tanh_cell", bufs=4)
             nc.scalar.activation(out=tanh_cell[u][:], in_=new_cell[u][:], func=ACT.Tanh)
 
         def finish_hidden(u):
             n, hb = divmod(u, H_BLOCKS)
             b, f0 = where(n)
-            new_hidden[u] = work.tile([P, TILE], F32, name="new_hidden", bufs=3)
-            nc.vector.tensor_tensor(out=new_hidden[u][:], in0=gate_out[u, "o"][:], in1=tanh_cell[u][:], op=ALU.mult)
+            new_hidden[u] = work.tile([P, TILE], F32, name="new_hidden", bufs=5)
+            shares = 2 if u == UNITS - 1 else 1
+            width = TILE // shares
+            for share in range(shares):
+                columns = slice(share * width, (share + 1) * width)
+                nc.vector.tensor_tensor(
+                    out=new_hidden[u][:, columns], in0=gate_out[u, "o"][:, columns], in1=tanh_cell[u][:, columns], op=ALU.mult
+                )
             nc.sync.dma_start(out=out_1[b, hb * P : (hb + 1) * P, f0 : f0 + TILE], in_=new_hidden[u][:])
 
         def turn_hidden(u):
+            if u == UNITS - 1:
+                turned_hidden[u] = [turn_psum.tile([P, 2, P], F32, tag="turn", name="turned_hidden") for share in range(2)]
+                for j in range(ROW_BLOCKS):
+                    nc.tensor.transpose(turned_hidden[u][j // 2][:, j % 2, :], new_hidden[u][:, j * P : (j + 1) * P], identity[:])
+                return
             turned_hidden[u] = turn_psum.tile([P, ROW_BLOCKS, P], F32, tag="turn", name="turned_hidden")
             for j in range(ROW_BLOCKS):
                 nc.tensor.transpose(turned_hidden[u][:, j, :], new_hidden[u][:, j * P : (j + 1) * P], identity[:])
@@ -237,7 +248,17 @@ def tile_batchedlstm_kernel(
         def copy_turned_hidden(u):
             n, hb = divmod(u, H_BLOCKS)
             b, f0 = where(n)
-            by_position = work.tile([P, ROW_BLOCKS, P], F32, name="by_position", bufs=3)
+            if u == UNITS - 1:
+                for share, copy_out in enumerate((nc.scalar.copy, nc.vector.tensor_copy)):
+                    half_by_position = work.tile([P, 2, P], F32, name="by_position", bufs=5)
+                    copy_out(out=half_by_position[:], in_=turned_hidden[u][share][:])
+                    first = f0 + share * HALF
+                    nc.sync.dma_start(
+                        out=out_0[b, first : first + HALF, hb * P : (hb + 1) * P].rearrange("(j p) h -> p j h", p=P),
+                        in_=half_by_position[:],
+                    )
+                return
+            by_position = work.tile([P, ROW_BLOCKS, P], F32, name="by_position", bufs=5)
             if u in SPLIT_COPIES:
                 nc.scalar.copy(out=by_position[:, 0:2, :], in_=turned_hidden[u][:, 0:2, :])
                 nc.vector.tensor_copy(out=by_position[:, 2:4, :], in_=turned_hidden[u][:, 2:4, :])
@@ -313,6 +334,10 @@ def tile_batchedlstm_kernel(
         bias_columns = keep.tile([P, len(GATES) * H_BLOCKS], F32, name="bias_columns")
         nc.vector.tensor_copy(out=bias_columns[:], in_=turned_bias[:, 0 : len(GATES) * H_BLOCKS])
 
+        def keep_warm_behind(tile_just_written):
+            nc.tensor.matmul(out=end_bank[0][:, 0:P], lhsT=identity[:], rhs=tile_just_written[:, 0:P], start=True, stop=True)
+
+        end_bank = []
         for u in range(-1, UNITS + 3):
             next_tile, quarter = divmod(u + PREPARE_AHEAD, H_BLOCKS)
             preparing = 1 <= next_tile < TILES
@@ -334,6 +359,8 @@ def tile_batchedlstm_kernel(
                 quantise(next_tile, 0, grouped_x[next_tile])
             if 0 <= u - 1 < UNITS:
                 finish_cell(u - 1)
+            if u == UNITS - 1:
+                end_bank.append(gate_psum.tile([P, TILE], F32, tag="pre", name="end_bank"))
             if 0 <= u < UNITS:
                 activate(u, "f")
             if 0 <= u - 2 < UNITS:
@@ -342,6 +369,9 @@ def tile_batchedlstm_kernel(
                 activate(u, "i")
                 keep_old_cell(u)
                 activate(u, "g")
+            if u == UNITS - 1:
+                for gate in ("f", "i", "g"):
+                    keep_warm_behind(gate_out[u, gate])
             if next_tile == 1 and quarter in (1, 2):
                 copy_x(1, quarter - 1)
             if 2 <= next_tile < TILES and quarter in (0, 2):
@@ -358,7 +388,11 @@ def tile_batchedlstm_kernel(
             if 0 <= u < UNITS:
                 activate(u, "o")
                 make_fresh(u)
+            if u == UNITS - 1:
+                keep_warm_behind(gate_out[u, "o"])
             if 0 <= u - 1 < UNITS:
                 squash_cell(u - 1)
+            if u - 1 in (UNITS - 2, UNITS - 1):
+                keep_warm_behind(tanh_cell[u - 1])
             if 0 <= u - 3 < UNITS:
                 copy_turned_hidden(u - 3)

from contextlib import ExitStack

import concourse.mybir as mybir
from concourse.masks import make_identity

F32 = mybir.dt.float32
BF16 = mybir.dt.bfloat16
I32 = mybir.dt.int32
U32 = mybir.dt.uint32
U8 = mybir.dt.uint8
FP8X4 = mybir.dt.float8_e4m3fn_x4
ACT = mybir.ActivationFunctionType
ALU = mybir.AluOpType

P = 128
PACK = 4
BATCH, POSITIONS, CHANNELS, HIDDEN = 2, 1024, 512, 512
PASSES = 2
PASS_ORDER = (1, 0)
TILE = 512
TILES_PER_BATCH = POSITIONS // TILE
TILES = BATCH * TILES_PER_BATCH
H_BLOCKS = HIDDEN // P
UNITS = TILES * H_BLOCKS
ROW_BLOCKS = TILE // P
HALF = TILE // 2
GATES = ("f", "i", "g", "o")
GATE_FUNC = {"f": ACT.Sigmoid, "i": ACT.Sigmoid, "g": ACT.Tanh, "o": ACT.Sigmoid}
QUADRANTS = 4
PREPARE_AHEAD = 4
LOAD_AHEAD = 5
WARM_AT_START = 4
SPLIT_COPIES = (0, 2, 4, 6, 8)
W_PART = 256

FLOPS = 2 * len(GATES) * HIDDEN * (CHANNELS + HIDDEN) * BATCH * POSITIONS


def tile_batchedlstm_kernel(
    tc,
    x,
    hidden_state,
    cell_state,
    W_f_words,
    W_f_scales,
    b_f,
    W_i_words,
    W_i_scales,
    b_i,
    W_o_words,
    W_o_scales,
    b_o,
    W_g_words,
    W_g_scales,
    b_g,
    out_0,
    out_1,
    out_2,
):
    nc = tc.nc
    words_in = {"f": W_f_words, "i": W_i_words, "g": W_g_words, "o": W_o_words}
    scales_in = {"f": W_f_scales, "i": W_i_scales, "g": W_g_scales, "o": W_o_scales}
    bias_in = {"f": b_f, "i": b_i, "g": b_g, "o": b_o}

    with ExitStack() as ctx:
        keep = ctx.enter_context(tc.tile_pool(name="keep", bufs=1))
        work = ctx.enter_context(tc.tile_pool(name="work", bufs=2))
        gate_psum = ctx.enter_context(tc.psum_pool(name="gate_psum", bufs=5))
        turn_psum = ctx.enter_context(tc.psum_pool(name="turn_psum", bufs=3))
        ctx.enter_context(tc.manual_schedule())

        def where(tile_index):
            return tile_index // TILES_PER_BATCH, (tile_index % TILES_PER_BATCH) * TILE

        x_rows = {
            (n, half): keep.tile([P, HALF // P, CHANNELS], BF16, name="x_rows%d%d" % (n, half))
            for n in range(TILES)
            for half in range(2)
        }
        hidden_rows = [keep.tile([P, PACK, TILE], BF16, name="hidden_rows%d" % n) for n in range(TILES)]
        xh_codes = [keep.tile([P, PASSES, TILE], U32, name="xh_codes%d" % n, align_bytes=64) for n in range(TILES)]
        xh_scales = [keep.tile([P, PASSES, TILE], U8, name="xh_scales%d" % n, align_bytes=64) for n in range(TILES)]
        cell_rows = {
            (b, hb): keep.tile([P, POSITIONS], BF16, name="cell_rows%d%d" % (b, hb))
            for b in range(BATCH)
            for hb in range(H_BLOCKS)
        }
        w_codes = {
            (gate, part): keep.tile([P, PASSES, W_PART], U32, name="w_codes_%s%d" % (gate, part), align_bytes=64)
            for gate in GATES
            for part in range(HIDDEN // W_PART)
        }
        w_scales = {gate: keep.tile([P, HIDDEN], U8, name="w_scales_%s" % gate, align_bytes=64) for gate in GATES}

        def load_x(n, half):
            b, f0 = where(n)
            first = f0 + half * HALF
            nc.sync.dma_start(out=x_rows[n, half][:], in_=x[b, first : first + HALF, :].rearrange("(j p) c -> p j c", p=P))

        def load_hidden(n):
            b, f0 = where(n)
            nc.sync.dma_start(
                out=hidden_rows[n][:],
                in_=hidden_state[b, :, f0 : f0 + TILE].rearrange("(p t) f -> p t f", t=PACK),
            )

        def load_weight_scales(gate):
            for quadrant in range(QUADRANTS):
                nc.sync.dma_start(
                    out=w_scales[gate][32 * quadrant : 32 * quadrant + PASSES * 4, :].bitcast(I32),
                    in_=scales_in[gate][:, 4 * quadrant : 4 * quadrant + 4, :].bitcast(I32),
                )

        def load_weight_codes(gate, part):
            all_bytes = words_in[gate].rearrange("c p n t -> p c (n t)")
            nc.sync.dma_start(
                out=w_codes[gate, part][:].bitcast(I32),
                in_=all_bytes[:, :, part * W_PART * PACK : (part + 1) * W_PART * PACK].bitcast(I32),
            )

        def load_cell(b, hb):
            nc.sync.dma_start(out=cell_rows[b, hb][:], in_=cell_state[b, hb * P : (hb + 1) * P, :])

        grouped_x = {}
        grouped_hidden = {}
        turned_x = {}

        def turn_x_block(n, block):
            half, j = divmod(block, 2)
            if j == 0:
                turned_x[n, half] = turn_psum.tile([P, 2, 2, P], F32, tag="turn", name="turned_x")
            words = x_rows[n, half][:, j, :].bitcast(F32)
            for u in range(2):
                nc.tensor.transpose(turned_x[n, half][:, j, u, :], words[:, u : CHANNELS // 2 : 2], identity[:])

        def turn_x(n, half):
            turn_x_block(n, 2 * half)
            turn_x_block(n, 2 * half + 1)

        def copy_x(n, half):
            if half == 0:
                grouped_x[n] = work.tile([P, TILE, PACK], BF16, name="grouped_x", align_bytes=64)
            as_words = grouped_x[n][:].bitcast(F32).rearrange("p (j f) u -> p j f u", f=P)
            nc.scalar.copy(
                out=as_words[:, 2 * half : 2 * half + 2, :, :],
                in_=turned_x[n, half][:].rearrange("p j u f -> p j f u"),
            )

        def regroup_hidden(n, half):
            if half == 0:
                grouped_hidden[n] = work.tile([P, TILE, PACK], BF16, name="grouped_hidden", align_bytes=64)
            columns = slice(half * HALF, (half + 1) * HALF)
            nc.vector.tensor_copy(
                out=grouped_hidden[n][:, columns, :].rearrange("p (c i) t -> p c t i", i=4),
                in_=hidden_rows[n][:, :, columns].rearrange("p t (c i) -> p c t i", i=4),
            )

        def quantise(n, c, grouped):
            nc.vector.quantize_mx(
                out=xh_codes[n][:, c, :].bitcast(FP8X4),
                scales=xh_scales[n][:, c, :],
                in_=grouped[:].rearrange("p f t -> p (f t)"),
            )

        pre = {}
        gate_out = {}
        kept = {}
        fresh = {}
        tanh_cell = {}
        new_cell = {}
        new_hidden = {}
        turned_hidden = {}

        def multiply(u):
            n, hb = divmod(u, H_BLOCKS)
            part, first = divmod(hb * P, W_PART)
            for gate in GATES:
                pre[u, gate] = gate_psum.tile([P, TILE], F32, tag="pre", name="pre_" + gate)
                for c in PASS_ORDER:
                    nc.tensor.matmul_mx(
                        out=pre[u, gate][:],
                        lhsT=w_codes[gate, part][:, c, first : first + P].bitcast(FP8X4),
                        lhsT_scale=w_scales[gate][4 * c : P, hb * P : (hb + 1) * P],
                        rhs=xh_codes[n][:, c, :].bitcast(FP8X4),
                        rhs_scale=xh_scales[n][:, c, :],
                        start=(c == PASS_ORDER[0]),
                        stop=(c == PASS_ORDER[-1]),
                    )

        def activate(u, gate):
            hb = u % H_BLOCKS
            column = GATES.index(gate) * H_BLOCKS + hb
            gate_out[u, gate] = work.tile([P, TILE], F32, name="gate_" + gate, bufs=4)
            nc.scalar.activation(
                out=gate_out[u, gate][:],
                in_=pre[u, gate][:],
                func=GATE_FUNC[gate],
                bias=bias_columns[:, column : column + 1],
                scale=1.0,
            )

        def keep_old_cell(u):
            n, hb = divmod(u, H_BLOCKS)
            b, f0 = where(n)
            kept[u] = work.tile([P, TILE], F32, name="kept", bufs=4)
            nc.vector.tensor_tensor(
                out=kept[u][:], in0=gate_out[u, "f"][:], in1=cell_rows[b, hb][:, f0 : f0 + TILE], op=ALU.mult
            )

        def make_fresh(u):
            fresh[u] = work.tile([P, TILE], F32, name="fresh", bufs=4)
            nc.vector.tensor_tensor(out=fresh[u][:], in0=gate_out[u, "i"][:], in1=gate_out[u, "g"][:], op=ALU.mult)

        def finish_cell(u):
            n, hb = divmod(u, H_BLOCKS)
            b, f0 = where(n)
            new_cell[u] = work.tile([P, TILE], F32, name="new_cell", bufs=5)
            nc.vector.tensor_tensor(out=new_cell[u][:], in0=kept[u][:], in1=fresh[u][:], op=ALU.add)
            nc.sync.dma_start(out=out_2[b, hb * P : (hb + 1) * P, f0 : f0 + TILE], in_=new_cell[u][:])

        def squash_cell(u):
            tanh_cell[u] = work.tile([P, TILE], F32, name="tanh_cell", bufs=4)
            nc.scalar.activation(out=tanh_cell[u][:], in_=new_cell[u][:], func=ACT.Tanh)

        def finish_hidden(u):
            n, hb = divmod(u, H_BLOCKS)
            b, f0 = where(n)
            new_hidden[u] = work.tile([P, TILE], F32, name="new_hidden", bufs=5)
            shares = 2 if u == UNITS - 1 else 1
            width = TILE // shares
            for share in range(shares):
                columns = slice(share * width, (share + 1) * width)
                nc.vector.tensor_tensor(
                    out=new_hidden[u][:, columns], in0=gate_out[u, "o"][:, columns], in1=tanh_cell[u][:, columns], op=ALU.mult
                )
            nc.sync.dma_start(out=out_1[b, hb * P : (hb + 1) * P, f0 : f0 + TILE], in_=new_hidden[u][:])

        def turn_hidden(u):
            if u == UNITS - 1:
                turned_hidden[u] = [turn_psum.tile([P, 2, P], F32, tag="turn", name="turned_hidden") for share in range(2)]
                for j in range(ROW_BLOCKS):
                    nc.tensor.transpose(turned_hidden[u][j // 2][:, j % 2, :], new_hidden[u][:, j * P : (j + 1) * P], identity[:])
                return
            turned_hidden[u] = turn_psum.tile([P, ROW_BLOCKS, P], F32, tag="turn", name="turned_hidden")
            for j in range(ROW_BLOCKS):
                nc.tensor.transpose(turned_hidden[u][:, j, :], new_hidden[u][:, j * P : (j + 1) * P], identity[:])

        def copy_turned_hidden(u):
            n, hb = divmod(u, H_BLOCKS)
            b, f0 = where(n)
            if u == UNITS - 1:
                for share, copy_out in enumerate((nc.scalar.copy, nc.vector.tensor_copy)):
                    half_by_position = work.tile([P, 2, P], F32, name="by_position", bufs=5)
                    copy_out(out=half_by_position[:], in_=turned_hidden[u][share][:])
                    first = f0 + share * HALF
                    nc.sync.dma_start(
                        out=out_0[b, first : first + HALF, hb * P : (hb + 1) * P].rearrange("(j p) h -> p j h", p=P),
                        in_=half_by_position[:],
                    )
                return
            by_position = work.tile([P, ROW_BLOCKS, P], F32, name="by_position", bufs=5)
            if u in SPLIT_COPIES:
                nc.scalar.copy(out=by_position[:, 0:2, :], in_=turned_hidden[u][:, 0:2, :])
                nc.vector.tensor_copy(out=by_position[:, 2:4, :], in_=turned_hidden[u][:, 2:4, :])
            else:
                nc.vector.tensor_copy(out=by_position[:], in_=turned_hidden[u][:])
            nc.sync.dma_start(
                out=out_0[b, f0 : f0 + TILE, hb * P : (hb + 1) * P].rearrange("(j p) h -> p j h", p=P), in_=by_position[:]
            )

        zeros = keep.tile([P, TILE], BF16, name="zeros")
        nc.vector.memset(zeros[:], 0.0)
        idle_bank = gate_psum.tile([P, TILE], F32, tag="pre", name="idle_bank")

        def keep_warm(moving, count):
            for k in range(count):
                nc.tensor.matmul(out=idle_bank[:], lhsT=zeros[:, 0:P], rhs=moving, start=True, stop=True)

        keep_warm(zeros[:], WARM_AT_START)
        bias_rows = keep.tile([P, P], BF16, name="bias_rows")
        nc.vector.memset(bias_rows[:], 0.0)
        for gate in GATES:
            nc.vector.memset(w_scales[gate][:].bitcast(I32), 0)
        identity = keep.tile([P, P], F32, name="identity")
        make_identity(nc, identity[:])
        identity_bf16 = keep.tile([P, P], BF16, name="identity_bf16")

        for row, gate in enumerate(GATES):
            nc.gpsimd.dma_start(
                out=bias_rows[row * H_BLOCKS : (row + 1) * H_BLOCKS, :], in_=bias_in[gate].rearrange("(hb h) -> hb h", h=P)
            )
        make_identity(nc, identity_bf16[:])
        warm = keep.tile([P, 1], F32, name="warm")
        nc.vector.memset(warm[:], 0.0)
        nc.scalar.activation(out=warm[:], in_=warm[:], func=ACT.Sigmoid)

        load_x(0, 0)
        load_x(0, 1)
        load_weight_scales("f")
        load_weight_codes("f", 0)
        load_hidden(0)
        for gate in ("i", "g", "o"):
            load_weight_scales(gate)
            load_weight_codes(gate, 0)
        load_cell(0, 0)
        load_hidden(1)
        load_x(1, 0)
        load_x(1, 1)
        load_cell(0, 1)
        for gate in GATES:
            load_weight_codes(gate, 1)
        load_cell(0, 2)
        load_cell(0, 3)

        def quarter_of(grouped, half):
            return grouped[:, half * HALF : half * HALF + TILE // PACK, :].rearrange("p f t -> p (f t)")

        turn_x(0, 0)
        copy_x(0, 0)
        turn_x(0, 1)
        copy_x(0, 1)
        keep_warm(quarter_of(grouped_x[0], 0), 2)
        keep_warm(quarter_of(grouped_x[0], 1), 2)
        regroup_hidden(0, 0)
        regroup_hidden(0, 1)
        keep_warm(quarter_of(grouped_hidden[0], 0), 2)
        keep_warm(quarter_of(grouped_hidden[0], 1), 2)

        turned_bias = turn_psum.tile([P, P], BF16, tag="turn", name="turned_bias")
        nc.tensor.transpose(turned_bias[:], bias_rows[:], identity_bf16[:])

        quantise(0, 1, grouped_hidden[0])
        quantise(0, 0, grouped_x[0])
        bias_columns = keep.tile([P, len(GATES) * H_BLOCKS], F32, name="bias_columns")
        nc.vector.tensor_copy(out=bias_columns[:], in_=turned_bias[:, 0 : len(GATES) * H_BLOCKS])

        def keep_warm_behind(tile_just_written):
            nc.tensor.matmul(out=end_bank[0][:, 0:P], lhsT=identity[:], rhs=tile_just_written[:, 0:P], start=True, stop=True)

        end_bank = []
        for u in range(-1, UNITS + 3):
            next_tile, quarter = divmod(u + PREPARE_AHEAD, H_BLOCKS)
            preparing = 1 <= next_tile < TILES
            tile_to_load, load_quarter = divmod(u + PREPARE_AHEAD + LOAD_AHEAD, H_BLOCKS)
            unit_to_load = u + LOAD_AHEAD

            if load_quarter == 0 and 2 <= tile_to_load < TILES:
                load_hidden(tile_to_load)
                load_x(tile_to_load, 0)
                load_x(tile_to_load, 1)
            if UNITS // BATCH <= unit_to_load < UNITS // BATCH + H_BLOCKS:
                load_cell(1, unit_to_load % H_BLOCKS)

            if preparing and quarter in (0, 1):
                regroup_hidden(next_tile, quarter)
            if preparing and quarter == 2:
                quantise(next_tile, 1, grouped_hidden[next_tile])
            if preparing and quarter == 3:
                quantise(next_tile, 0, grouped_x[next_tile])
            if 0 <= u - 1 < UNITS:
                finish_cell(u - 1)
            if u == UNITS - 1:
                end_bank.append(gate_psum.tile([P, TILE], F32, tag="pre", name="end_bank"))
            if 0 <= u < UNITS:
                activate(u, "f")
            if 0 <= u - 2 < UNITS:
                finish_hidden(u - 2)
            if 0 <= u < UNITS:
                activate(u, "i")
                keep_old_cell(u)
                activate(u, "g")
            if u == UNITS - 1:
                for gate in ("f", "i", "g"):
                    keep_warm_behind(gate_out[u, gate])
            if next_tile == 1 and quarter in (1, 2):
                copy_x(1, quarter - 1)
            if 2 <= next_tile < TILES and quarter in (0, 2):
                copy_x(next_tile, quarter // 2)
            if u + 1 < UNITS:
                multiply(u + 1)
            if 0 <= u - 2 < UNITS:
                turn_hidden(u - 2)
            if next_tile == 1 and quarter in (0, 1):
                turn_x(1, quarter)
            tile_to_turn, block = divmod(u + PREPARE_AHEAD + 2, H_BLOCKS)
            if 2 <= tile_to_turn < TILES:
                turn_x_block(tile_to_turn, block)
            if 0 <= u < UNITS:
                activate(u, "o")
                make_fresh(u)
            if u == UNITS - 1:
                keep_warm_behind(gate_out[u, "o"])
            if 0 <= u - 1 < UNITS:
                squash_cell(u - 1)
            if u - 1 in (UNITS - 2, UNITS - 1):
                keep_warm_behind(tanh_cell[u - 1])
            if 0 <= u - 3 < UNITS:
                copy_turned_hidden(u - 3)
